import numpy as np
import ml_dtypes

BF16 = ml_dtypes.bfloat16


def bf(x):
    return np.asarray(x, np.float32).astype(BF16)


def f32(x):
    return np.asarray(x, np.float32)


def f64(x):
    return np.asarray(x).astype(np.float64)


def striped(idx):
    return np.tile(idx.reshape(-1, 16).T, (8, 1))


V, D, N = 1024, 128, 512


def setup_inputs():
    return {
        "table": bf(0.1 * np.random.standard_normal((D, V))),
        "wq": bf(np.random.standard_normal((D, D)) / np.sqrt(D)),
        "bq": f32(0.1 * np.random.standard_normal((D, 1))),
        "wke": bf(np.random.standard_normal((D, D)) / np.sqrt(D)),
        "bke": f32(0.1 * np.random.standard_normal((D, 1))),
        "wv": bf(np.random.standard_normal((D, D)) / np.sqrt(D)),
        "bv": f32(0.1 * np.random.standard_normal((D, 1))),
        "offs": striped(np.random.permutation(np.tile(np.arange(V), 2))[:N]),
    }


def reference(table, wq, bq, wke, bke, wv, bv, offs):
    idx = offs[:16].T.reshape(-1)
    picked = f64(table)[:, idx]
    scale = np.sqrt(D)
    return np.concatenate([
        scale * picked,
        scale * (f64(wq).T @ picked) + f64(bq),
        scale * (f64(wke).T @ picked) + f64(bke),
        scale * (f64(wv).T @ picked) + f64(bv),
    ], axis=0)

@@ -1,0 +1,48 @@
+import math
+
+import concourse.mybir as mybir
+from concourse.masks import make_identity
+
+P = 128
+V = 1024
+N = 512
+BF16, F32, U16 = mybir.dt.bfloat16, mybir.dt.float32, mybir.dt.uint16
+SCALE = math.sqrt(float(P))
+FLOPS = 3 * 2 * P * P * N
+
+
+def tile_transformer_xl_kernel(tc, table, wq, bq, wke, bke, wv, bv, offs, out):
+    nc = tc.nc
+    mult, add = mybir.AluOpType.mult, mybir.AluOpType.add
+    identity_fn = mybir.ActivationFunctionType.Identity
+
+    with tc.tile_pool(name="held", bufs=1) as held, tc.psum_pool(name="psum", bufs=1) as psum:
+        offsets = held.tile([P, N // 16], U16, name="offsets")
+        nc.sync.dma_start(offsets[:], offs)
+        words = held.tile([P, V], BF16, name="words")
+        nc.sync.dma_start(words[:], table)
+
+        eye = held.tile([P, P], BF16, name="eye")
+        make_identity(nc, eye[:])
+        weights = [eye]
+        biases = [None]
+        for name, w_dram, b_dram in (("q", wq, bq), ("ke", wke, bke), ("v", wv, bv)):
+            w_tile = held.tile([P, P], BF16, name="w_" + name)
+            nc.scalar.dma_start(w_tile[:], w_dram)
+            b_tile = held.tile([P, 1], F32, name="b_" + name)
+            nc.sync.dma_start(b_tile[:], b_dram)
+            weights.append(w_tile)
+            biases.append(b_tile)
+
+        for block in range(4):
+            product = psum.tile([P, N], F32, name="product" + str(block))
+            nc.tensor.matmul(product[:], weights[block][:], words[:].indirect(offsets[:]), start=True, stop=True)
+
+            staged = held.tile([P, N], F32, name="staged" + str(block))
+            if block == 0:
+                nc.vector.tensor_scalar(staged[:], product[:], SCALE, None, mult)
+            elif block % 2 == 0:
+                nc.vector.tensor_scalar(staged[:], product[:], SCALE, biases[block][:], mult, add)
+            else:
+                nc.scalar.activation(staged[:], product[:], identity_fn, bias=biases[block][:], scale=SCALE)
+            nc.sync.dma_start(out[block * P : (block + 1) * P, :], staged[:])

@@ -8,6 +8,7 @@ V = 1024
 N = 512
 BF16, F32, U16 = mybir.dt.bfloat16, mybir.dt.float32, mybir.dt.uint16
 SCALE = math.sqrt(float(P))
+WARM_UP = 6
 FLOPS = 3 * 2 * P * P * N
 
 
@@ -33,6 +34,16 @@ def tile_transformer_xl_kernel(tc, table, wq, bq, wke, bke, wv, bv, offs, out):
             nc.sync.dma_start(b_tile[:], b_dram)
             weights.append(w_tile)
             biases.append(b_tile)
+
+        zeros = held.tile([P, N], BF16, name="zeros")
+        nc.vector.memset(zeros[:], 0.0)
+        unread = psum.tile([P, N], F32, name="unread")
+        for turn in range(WARM_UP):
+            nc.tensor.matmul(unread[:], zeros[:, 0:P], zeros[:], start=True, stop=True)
+
+        scratch = held.tile([P, 1], F32, name="scratch")
+        nc.vector.memset(scratch[:], 0.0)
+        nc.scalar.activation(scratch[:], scratch[:], identity_fn)
 
         for block in range(4):
             product = psum.tile([P, N], F32, name="product" + str(block))

@@ -6,9 +6,9 @@ from concourse.masks import make_identity
 P = 128
 V = 1024
 N = 512
+PIECE = N // 2
 BF16, F32, U16 = mybir.dt.bfloat16, mybir.dt.float32, mybir.dt.uint16
 SCALE = math.sqrt(float(P))
-WARM_UP = 6
 FLOPS = 3 * 2 * P * P * N
 
 
@@ -25,8 +25,10 @@ def tile_transformer_xl_kernel(tc, table, wq, bq, wke, bke, wv, bv, offs, out):
 
         eye = held.tile([P, P], BF16, name="eye")
         make_identity(nc, eye[:])
+        no_bias = held.tile([P, 1], F32, name="no_bias")
+        nc.vector.memset(no_bias[:], 0.0)
         weights = [eye]
-        biases = [None]
+        biases = [no_bias]
         for name, w_dram, b_dram in (("q", wq, bq), ("ke", wke, bke), ("v", wv, bv)):
             w_tile = held.tile([P, P], BF16, name="w_" + name)
             nc.scalar.dma_start(w_tile[:], w_dram)
@@ -35,25 +37,19 @@ def tile_transformer_xl_kernel(tc, table, wq, bq, wke, bke, wv, bv, offs, out):
             weights.append(w_tile)
             biases.append(b_tile)
 
-        zeros = held.tile([P, N], BF16, name="zeros")
-        nc.vector.memset(zeros[:], 0.0)
-        unread = psum.tile([P, N], F32, name="unread")
-        for turn in range(WARM_UP):
-            nc.tensor.matmul(unread[:], zeros[:, 0:P], zeros[:], start=True, stop=True)
-
         scratch = held.tile([P, 1], F32, name="scratch")
-        nc.vector.memset(scratch[:], 0.0)
-        nc.scalar.activation(scratch[:], scratch[:], identity_fn)
+        nc.scalar.activation(scratch[:], no_bias[:], identity_fn)
 
         for block in range(4):
-            product = psum.tile([P, N], F32, name="product" + str(block))
-            nc.tensor.matmul(product[:], weights[block][:], words[:].indirect(offsets[:]), start=True, stop=True)
-
             staged = held.tile([P, N], F32, name="staged" + str(block))
-            if block == 0:
-                nc.vector.tensor_scalar(staged[:], product[:], SCALE, None, mult)
-            elif block % 2 == 0:
-                nc.vector.tensor_scalar(staged[:], product[:], SCALE, biases[block][:], mult, add)
-            else:
-                nc.scalar.activation(staged[:], product[:], identity_fn, bias=biases[block][:], scale=SCALE)
-            nc.sync.dma_start(out[block * P : (block + 1) * P, :], staged[:])
+            for piece in range(N // PIECE):
+                columns = slice(piece * PIECE, (piece + 1) * PIECE)
+                looked_up = words[:].indirect(offsets[:, piece * (PIECE // 16) : (piece + 1) * (PIECE // 16)])
+                product = psum.tile([P, PIECE], F32, name="product" + str(block) + str(piece))
+                nc.tensor.matmul(product[:], weights[block][:], looked_up, start=True, stop=True)
+
+                if piece == 0:
+                    nc.vector.tensor_scalar(staged[:, columns], product[:], SCALE, biases[block][:], mult, add)
+                else:
+                    nc.scalar.activation(staged[:, columns], product[:], identity_fn, bias=biases[block][:], scale=SCALE)
+                nc.sync.dma_start(out[block * P : (block + 1) * P, columns], staged[:, columns])

@@ -9,6 +9,8 @@ N = 512
 PIECE = N // 2
 BF16, F32, U16 = mybir.dt.bfloat16, mybir.dt.float32, mybir.dt.uint16
 SCALE = math.sqrt(float(P))
+CLOCK_BAR = 1024
+WARM_UP = 2 * CLOCK_BAR // P
 FLOPS = 3 * 2 * P * P * N
 
 
@@ -17,7 +19,13 @@ def tile_transformer_xl_kernel(tc, table, wq, bq, wke, bke, wv, bv, offs, out):
     mult, add = mybir.AluOpType.mult, mybir.AluOpType.add
     identity_fn = mybir.ActivationFunctionType.Identity
 
-    with tc.tile_pool(name="held", bufs=1) as held, tc.psum_pool(name="psum", bufs=1) as psum:
+    with tc.tile_pool(name="held", bufs=1) as held, tc.psum_pool(name="psum", bufs=8) as psum:
+        zeros = held.tile([P, P], BF16, name="zeros")
+        nc.vector.memset(zeros[:], 0.0)
+        unread = psum.tile([P, P], F32, name="unread", tag="bank")
+        for turn in range(WARM_UP):
+            nc.tensor.matmul(unread[:], zeros[:], zeros[:], start=True, stop=True)
+
         offsets = held.tile([P, N // 16], U16, name="offsets")
         nc.sync.dma_start(offsets[:], offs)
         words = held.tile([P, V], BF16, name="words")
@@ -45,7 +53,7 @@ def tile_transformer_xl_kernel(tc, table, wq, bq, wke, bke, wv, bv, offs, out):
             for piece in range(N // PIECE):
                 columns = slice(piece * PIECE, (piece + 1) * PIECE)
                 looked_up = words[:].indirect(offsets[:, piece * (PIECE // 16) : (piece + 1) * (PIECE // 16)])
-                product = psum.tile([P, PIECE], F32, name="product" + str(block) + str(piece))
+                product = psum.tile([P, PIECE], F32, name="product", tag="bank")
                 nc.tensor.matmul(product[:], weights[block][:], looked_up, start=True, stop=True)
 
                 if piece == 0:

@@ -9,8 +9,6 @@ N = 512
 PIECE = N // 2
 BF16, F32, U16 = mybir.dt.bfloat16, mybir.dt.float32, mybir.dt.uint16
 SCALE = math.sqrt(float(P))
-CLOCK_BAR = 1024
-WARM_UP = 2 * CLOCK_BAR // P
 FLOPS = 3 * 2 * P * P * N
 
 
@@ -19,13 +17,7 @@ def tile_transformer_xl_kernel(tc, table, wq, bq, wke, bke, wv, bv, offs, out):
     mult, add = mybir.AluOpType.mult, mybir.AluOpType.add
     identity_fn = mybir.ActivationFunctionType.Identity
 
-    with tc.tile_pool(name="held", bufs=1) as held, tc.psum_pool(name="psum", bufs=8) as psum:
-        zeros = held.tile([P, P], BF16, name="zeros")
-        nc.vector.memset(zeros[:], 0.0)
-        unread = psum.tile([P, P], F32, name="unread", tag="bank")
-        for turn in range(WARM_UP):
-            nc.tensor.matmul(unread[:], zeros[:], zeros[:], start=True, stop=True)
-
+    with tc.tile_pool(name="held", bufs=1) as held, tc.psum_pool(name="psum", bufs=1) as psum:
         offsets = held.tile([P, N // 16], U16, name="offsets")
         nc.sync.dma_start(offsets[:], offs)
         words = held.tile([P, V], BF16, name="words")
@@ -39,7 +31,7 @@ def tile_transformer_xl_kernel(tc, table, wq, bq, wke, bke, wv, bv, offs, out):
         biases = [no_bias]
         for name, w_dram, b_dram in (("q", wq, bq), ("ke", wke, bke), ("v", wv, bv)):
             w_tile = held.tile([P, P], BF16, name="w_" + name)
-            nc.scalar.dma_start(w_tile[:], w_dram)
+            nc.sync.dma_start(w_tile[:], w_dram)
             b_tile = held.tile([P, 1], F32, name="b_" + name)
             nc.sync.dma_start(b_tile[:], b_dram)
             weights.append(w_tile)
@@ -53,7 +45,7 @@ def tile_transformer_xl_kernel(tc, table, wq, bq, wke, bke, wv, bv, offs, out):
             for piece in range(N // PIECE):
                 columns = slice(piece * PIECE, (piece + 1) * PIECE)
                 looked_up = words[:].indirect(offsets[:, piece * (PIECE // 16) : (piece + 1) * (PIECE // 16)])
-                product = psum.tile([P, PIECE], F32, name="product", tag="bank")
+                product = psum.tile([P, PIECE], F32, name="product" + str(block) + str(piece))
                 nc.tensor.matmul(product[:], weights[block][:], looked_up, start=True, stop=True)
 
                 if piece == 0:

@@ -7,6 +7,7 @@ P = 128
 V = 1024
 N = 512
 PIECE = N // 2
+BANKS = 8
 BF16, F32, U16 = mybir.dt.bfloat16, mybir.dt.float32, mybir.dt.uint16
 SCALE = math.sqrt(float(P))
 FLOPS = 3 * 2 * P * P * N
@@ -17,7 +18,7 @@ def tile_transformer_xl_kernel(tc, table, wq, bq, wke, bke, wv, bv, offs, out):
     mult, add = mybir.AluOpType.mult, mybir.AluOpType.add
     identity_fn = mybir.ActivationFunctionType.Identity
 
-    with tc.tile_pool(name="held", bufs=1) as held, tc.psum_pool(name="psum", bufs=1) as psum:
+    with tc.tile_pool(name="held", bufs=1) as held, tc.psum_pool(name="psum", bufs=BANKS) as psum:
         offsets = held.tile([P, N // 16], U16, name="offsets")
         nc.sync.dma_start(offsets[:], offs)
         words = held.tile([P, V], BF16, name="words")
@@ -45,7 +46,7 @@ def tile_transformer_xl_kernel(tc, table, wq, bq, wke, bke, wv, bv, offs, out):
             for piece in range(N // PIECE):
                 columns = slice(piece * PIECE, (piece + 1) * PIECE)
                 looked_up = words[:].indirect(offsets[:, piece * (PIECE // 16) : (piece + 1) * (PIECE // 16)])
-                product = psum.tile([P, PIECE], F32, name="product" + str(block) + str(piece))
+                product = psum.tile([P, PIECE], F32, name="product")
                 nc.tensor.matmul(product[:], weights[block][:], looked_up, start=True, stop=True)
 
                 if piece == 0:

@@ -16,7 +16,6 @@ FLOPS = 3 * 2 * P * P * N
 def tile_transformer_xl_kernel(tc, table, wq, bq, wke, bke, wv, bv, offs, out):
     nc = tc.nc
     mult, add = mybir.AluOpType.mult, mybir.AluOpType.add
-    identity_fn = mybir.ActivationFunctionType.Identity
 
     with tc.tile_pool(name="held", bufs=1) as held, tc.psum_pool(name="psum", bufs=BANKS) as psum:
         offsets = held.tile([P, N // 16], U16, name="offsets")
@@ -38,9 +37,6 @@ def tile_transformer_xl_kernel(tc, table, wq, bq, wke, bke, wv, bv, offs, out):
             weights.append(w_tile)
             biases.append(b_tile)
 
-        scratch = held.tile([P, 1], F32, name="scratch")
-        nc.scalar.activation(scratch[:], no_bias[:], identity_fn)
-
         for block in range(4):
             staged = held.tile([P, N], F32, name="staged" + str(block))
             for piece in range(N // PIECE):
@@ -49,8 +45,6 @@ def tile_transformer_xl_kernel(tc, table, wq, bq, wke, bke, wv, bv, offs, out):
                 product = psum.tile([P, PIECE], F32, name="product")
                 nc.tensor.matmul(product[:], weights[block][:], looked_up, start=True, stop=True)
 
-                if piece == 0:
-                    nc.vector.tensor_scalar(staged[:, columns], product[:], SCALE, biases[block][:], mult, add)
-                else:
-                    nc.scalar.activation(staged[:, columns], product[:], identity_fn, bias=biases[block][:], scale=SCALE)
-                nc.sync.dma_start(out[block * P : (block + 1) * P, columns], staged[:, columns])
+                nc.vector.tensor_scalar(staged[:, columns], product[:], SCALE, biases[block][:], mult, add)
+                store_queue = nc.sync if piece == 0 else nc.scalar
+                store_queue.dma_start(out[block * P : (block + 1) * P, columns], staged[:, columns])

@@ -46,5 +46,4 @@ def tile_transformer_xl_kernel(tc, table, wq, bq, wke, bke, wv, bv, offs, out):
                 nc.tensor.matmul(product[:], weights[block][:], looked_up, start=True, stop=True)
 
                 nc.vector.tensor_scalar(staged[:, columns], product[:], SCALE, biases[block][:], mult, add)
-                store_queue = nc.sync if piece == 0 else nc.scalar
-                store_queue.dma_start(out[block * P : (block + 1) * P, columns], staged[:, columns])
+                nc.sync.dma_start(out[block * P : (block + 1) * P, columns], staged[:, columns])

@@ -18,10 +18,10 @@ def tile_transformer_xl_kernel(tc, table, wq, bq, wke, bke, wv, bv, offs, out):
     mult, add = mybir.AluOpType.mult, mybir.AluOpType.add
 
     with tc.tile_pool(name="held", bufs=1) as held, tc.psum_pool(name="psum", bufs=BANKS) as psum:
-        offsets = held.tile([P, N // 16], U16, name="offsets")
-        nc.sync.dma_start(offsets[:], offs)
         words = held.tile([P, V], BF16, name="words")
         nc.sync.dma_start(words[:], table)
+        offsets = held.tile([P, N // 16], U16, name="offsets")
+        nc.sync.dma_start(offsets[:], offs)
 
         eye = held.tile([P, P], BF16, name="eye")
         make_identity(nc, eye[:])

@@ -37,13 +37,13 @@ def tile_transformer_xl_kernel(tc, table, wq, bq, wke, bke, wv, bv, offs, out):
             weights.append(w_tile)
             biases.append(b_tile)
 
-        for block in range(4):
-            staged = held.tile([P, N], F32, name="staged" + str(block))
-            for piece in range(N // PIECE):
-                columns = slice(piece * PIECE, (piece + 1) * PIECE)
+        for piece in range(N // PIECE):
+            columns = slice(piece * PIECE, (piece + 1) * PIECE)
+            for block in range(4):
+                staged = held.tile([P, PIECE], F32, name="staged" + str(block) + str(piece))
                 looked_up = words[:].indirect(offsets[:, piece * (PIECE // 16) : (piece + 1) * (PIECE // 16)])
                 product = psum.tile([P, PIECE], F32, name="product")
                 nc.tensor.matmul(product[:], weights[block][:], looked_up, start=True, stop=True)
 
-                nc.vector.tensor_scalar(staged[:, columns], product[:], SCALE, biases[block][:], mult, add)
-                nc.sync.dma_start(out[block * P : (block + 1) * P, columns], staged[:, columns])
+                nc.vector.tensor_scalar(staged[:], product[:], SCALE, biases[block][:], mult, add)
+                nc.sync.dma_start(out[block * P : (block + 1) * P, columns], staged[:])

@@ -6,7 +6,8 @@ from concourse.masks import make_identity
 P = 128
 V = 1024
 N = 512
-PIECE = N // 2
+HALVES = (0, N // 2, N)
+THIRDS = (0, N // 4, N * 5 // 8, N)
 BANKS = 8
 BF16, F32, U16 = mybir.dt.bfloat16, mybir.dt.float32, mybir.dt.uint16
 SCALE = math.sqrt(float(P))
@@ -37,13 +38,13 @@ def tile_transformer_xl_kernel(tc, table, wq, bq, wke, bke, wv, bv, offs, out):
             weights.append(w_tile)
             biases.append(b_tile)
 
-        for piece in range(N // PIECE):
-            columns = slice(piece * PIECE, (piece + 1) * PIECE)
-            for block in range(4):
-                staged = held.tile([P, PIECE], F32, name="staged" + str(block) + str(piece))
-                looked_up = words[:].indirect(offsets[:, piece * (PIECE // 16) : (piece + 1) * (PIECE // 16)])
-                product = psum.tile([P, PIECE], F32, name="product")
+        for block in range(4):
+            cuts = THIRDS if block == 0 else HALVES
+            for start, stop in zip(cuts[:-1], cuts[1:]):
+                staged = held.tile([P, stop - start], F32, name="staged" + str(block) + "_" + str(start))
+                looked_up = words[:].indirect(offsets[:, start // 16 : stop // 16])
+                product = psum.tile([P, stop - start], F32, name="product")
                 nc.tensor.matmul(product[:], weights[block][:], looked_up, start=True, stop=True)
 
                 nc.vector.tensor_scalar(staged[:], product[:], SCALE, biases[block][:], mult, add)
-                nc.sync.dma_start(out[block * P : (block + 1) * P, columns], staged[:])
+                nc.sync.dma_start(out[block * P : (block + 1) * P, start:stop], staged[:])

@@ -7,7 +7,7 @@ P = 128
 V = 1024
 N = 512
 HALVES = (0, N // 2, N)
-THIRDS = (0, N // 4, N * 5 // 8, N)
+FIRST_CUTS = (0, N // 4, N * 5 // 8, N)
 BANKS = 8
 BF16, F32, U16 = mybir.dt.bfloat16, mybir.dt.float32, mybir.dt.uint16
 SCALE = math.sqrt(float(P))
@@ -17,6 +17,7 @@ FLOPS = 3 * 2 * P * P * N
 def tile_transformer_xl_kernel(tc, table, wq, bq, wke, bke, wv, bv, offs, out):
     nc = tc.nc
     mult, add = mybir.AluOpType.mult, mybir.AluOpType.add
+    identity_function = mybir.ActivationFunctionType.Identity
 
     with tc.tile_pool(name="held", bufs=1) as held, tc.psum_pool(name="psum", bufs=BANKS) as psum:
         words = held.tile([P, V], BF16, name="words")
@@ -38,13 +39,26 @@ def tile_transformer_xl_kernel(tc, table, wq, bq, wke, bke, wv, bv, offs, out):
             weights.append(w_tile)
             biases.append(b_tile)
 
+        early = held.tile([P, 1], F32, name="early")
+        nc.scalar.activation(early[:], no_bias[:], identity_function, bias=no_bias[:], scale=SCALE)
+
         for block in range(4):
-            cuts = THIRDS if block == 0 else HALVES
+            rows = slice(block * P, (block + 1) * P)
+            staged = held.tile([P, N], F32, name="staged" + str(block))
+            cuts = FIRST_CUTS if block == 0 else HALVES
+            stored_whole = block == 2
             for start, stop in zip(cuts[:-1], cuts[1:]):
-                staged = held.tile([P, stop - start], F32, name="staged" + str(block) + "_" + str(start))
                 looked_up = words[:].indirect(offsets[:, start // 16 : stop // 16])
                 product = psum.tile([P, stop - start], F32, name="product")
                 nc.tensor.matmul(product[:], weights[block][:], looked_up, start=True, stop=True)
 
-                nc.vector.tensor_scalar(staged[:], product[:], SCALE, biases[block][:], mult, add)
-                nc.sync.dma_start(out[block * P : (block + 1) * P, start:stop], staged[:])
+                if block >= 2 and stop == N:
+                    nc.scalar.activation(
+                        staged[:, start:stop], product[:], identity_function, bias=biases[block][:], scale=SCALE
+                    )
+                else:
+                    nc.vector.tensor_scalar(staged[:, start:stop], product[:], SCALE, biases[block][:], mult, add)
+                if not stored_whole:
+                    nc.sync.dma_start(out[rows, start:stop], staged[:, start:stop])
+            if stored_whole:
+                nc.sync.dma_start(out[rows, :], staged[:])

@@ -3,6 +3,7 @@ import math
 import concourse.mybir as mybir
 from concourse.masks import make_identity
 
+GROUP = 32
 P = 128
 V = 1024
 N = 512
@@ -25,27 +26,32 @@ def tile_transformer_xl_kernel(tc, table, wq, bq, wke, bke, wv, bv, offs, out):
         offsets = held.tile([P, N // 16], U16, name="offsets")
         nc.sync.dma_start(offsets[:], offs)
 
+        bias_rows = held.tile([P, GROUP], F32, name="bias_rows", align_bytes=64)
+        nc.vector.memset(bias_rows[:], 0.0)
+        for block, b_dram in ((1, bq), (2, bke), (3, bv)):
+            nc.sync.dma_start(bias_rows[block::GROUP, :], b_dram.rearrange("(g i) o -> g (i o)", i=GROUP))
+        bias_columns = held.tile([P, GROUP], F32, name="bias_columns", align_bytes=64)
+
         eye = held.tile([P, P], BF16, name="eye")
         make_identity(nc, eye[:])
-        no_bias = held.tile([P, 1], F32, name="no_bias")
-        nc.vector.memset(no_bias[:], 0.0)
         weights = [eye]
-        biases = [no_bias]
-        for name, w_dram, b_dram in (("q", wq, bq), ("ke", wke, bke), ("v", wv, bv)):
+        for name, w_dram in (("q", wq), ("ke", wke), ("v", wv)):
             w_tile = held.tile([P, P], BF16, name="w_" + name)
             nc.sync.dma_start(w_tile[:], w_dram)
-            b_tile = held.tile([P, 1], F32, name="b_" + name)
-            nc.sync.dma_start(b_tile[:], b_dram)
             weights.append(w_tile)
-            biases.append(b_tile)
 
+        zero = held.tile([P, 1], F32, name="zero")
+        nc.vector.memset(zero[:], 0.0)
         early = held.tile([P, 1], F32, name="early")
-        nc.scalar.activation(early[:], no_bias[:], identity_function, bias=no_bias[:], scale=SCALE)
+        nc.scalar.activation(early[:], zero[:], identity_function, bias=zero[:], scale=SCALE)
 
         for block in range(4):
             rows = slice(block * P, (block + 1) * P)
             staged = held.tile([P, N], F32, name="staged" + str(block))
             cuts = FIRST_CUTS if block == 0 else HALVES
+            if block == 1:
+                nc.vector.transpose(bias_columns[:], bias_rows[:])
+            bias = zero[:] if block == 0 else bias_columns[:, block : block + 1]
             stored_whole = block == 2
             for start, stop in zip(cuts[:-1], cuts[1:]):
                 looked_up = words[:].indirect(offsets[:, start // 16 : stop // 16])
@@ -54,10 +60,10 @@ def tile_transformer_xl_kernel(tc, table, wq, bq, wke, bke, wv, bv, offs, out):
 
                 if block >= 2 and stop == N:
                     nc.scalar.activation(
-                        staged[:, start:stop], product[:], identity_function, bias=biases[block][:], scale=SCALE
+                        staged[:, start:stop], product[:], identity_function, bias=bias, scale=SCALE
                     )
                 else:
-                    nc.vector.tensor_scalar(staged[:, start:stop], product[:], SCALE, biases[block][:], mult, add)
+                    nc.vector.tensor_scalar(staged[:, start:stop], product[:], SCALE, bias, mult, add)
                 if not stored_whole:
                     nc.sync.dma_start(out[rows, start:stop], staged[:, start:stop])
             if stored_whole:

import math

import concourse.mybir as mybir
from concourse.masks import make_identity

GROUP = 32
P = 128
V = 1024
N = 512
HALVES = (0, N // 2, N)
FIRST_CUTS = (0, N // 4, N * 5 // 8, N)
BANKS = 8
BF16, F32, U16 = mybir.dt.bfloat16, mybir.dt.float32, mybir.dt.uint16
SCALE = math.sqrt(float(P))
FLOPS = 3 * 2 * P * P * N


def tile_transformer_xl_kernel(tc, table, wq, bq, wke, bke, wv, bv, offs, out):
    nc = tc.nc
    mult, add = mybir.AluOpType.mult, mybir.AluOpType.add
    identity_function = mybir.ActivationFunctionType.Identity

    with tc.tile_pool(name="held", bufs=1) as held, tc.psum_pool(name="psum", bufs=BANKS) as psum:
        words = held.tile([P, V], BF16, name="words")
        nc.sync.dma_start(words[:], table)
        offsets = held.tile([P, N // 16], U16, name="offsets")
        nc.sync.dma_start(offsets[:], offs)

        bias_rows = held.tile([P, GROUP], F32, name="bias_rows", align_bytes=64)
        nc.vector.memset(bias_rows[:], 0.0)
        for block, b_dram in ((1, bq), (2, bke), (3, bv)):
            nc.sync.dma_start(bias_rows[block::GROUP, :], b_dram.rearrange("(g i) o -> g (i o)", i=GROUP))
        bias_columns = held.tile([P, GROUP], F32, name="bias_columns", align_bytes=64)

        eye = held.tile([P, P], BF16, name="eye")
        make_identity(nc, eye[:])
        weights = [eye]
        for name, w_dram in (("q", wq), ("ke", wke), ("v", wv)):
            w_tile = held.tile([P, P], BF16, name="w_" + name)
            nc.sync.dma_start(w_tile[:], w_dram)
            weights.append(w_tile)

        zero = held.tile([P, 1], F32, name="zero")
        nc.vector.memset(zero[:], 0.0)
        early = held.tile([P, 1], F32, name="early")
        nc.scalar.activation(early[:], zero[:], identity_function, bias=zero[:], scale=SCALE)

        for block in range(4):
            rows = slice(block * P, (block + 1) * P)
            staged = held.tile([P, N], F32, name="staged" + str(block))
            cuts = FIRST_CUTS if block == 0 else HALVES
            if block == 1:
                nc.vector.transpose(bias_columns[:], bias_rows[:])
            bias = zero[:] if block == 0 else bias_columns[:, block : block + 1]
            stored_whole = block == 2
            for start, stop in zip(cuts[:-1], cuts[1:]):
                looked_up = words[:].indirect(offsets[:, start // 16 : stop // 16])
                product = psum.tile([P, stop - start], F32, name="product")
                nc.tensor.matmul(product[:], weights[block][:], looked_up, start=True, stop=True)

                if block >= 2 and stop == N:
                    nc.scalar.activation(
                        staged[:, start:stop], product[:], identity_function, bias=bias, scale=SCALE
                    )
                else:
                    nc.vector.tensor_scalar(staged[:, start:stop], product[:], SCALE, bias, mult, add)
                if not stored_whole:
                    nc.sync.dma_start(out[rows, start:stop], staged[:, start:stop])
            if stored_whole:
                nc.sync.dma_start(out[rows, :], staged[:])
